import numpy as np
import ml_dtypes


BF16 = ml_dtypes.bfloat16


def bf(x):
    return np.asarray(x, np.float32).astype(BF16)


def f64(x):
    return np.asarray(x).astype(np.float64)


E2M1 = np.array([0.0, 0.5, 1.0, 1.5, 2.0, 3.0, 4.0, 6.0, -0.0, -0.5, -1.0, -1.5, -2.0, -3.0, -4.0, -6.0])


def pack_weight(w, fmt):
    k, n = w.shape
    w = f64(bf(w)).reshape(k // 32, 32, n)
    amax = np.abs(w).max(1)
    if fmt == "e4m3":
        byte = np.frexp(amax)[1] - 1 + 127 - 7
    else:
        mant, ex = np.frexp(amax / 6.0)
        byte = np.where(mant > 0.5, ex, ex - 1) + 127
    byte = np.clip(np.where(amax > 0, byte, 1), 1, 254)
    scaled = (w * np.exp2(127.0 - byte)[:, None, :]).reshape(k, n).astype(np.float32)
    by_word = np.ascontiguousarray(scaled.reshape(k // 512, 128, 4, n).transpose(0, 1, 3, 2))
    if fmt == "e4m3":
        words = by_word.astype(ml_dtypes.float8_e4m3fn).view(np.uint8)
    else:
        c = by_word.astype(ml_dtypes.float4_e2m1fn).view(np.uint8) & 0xF
        words = c[..., 0::2] | (c[..., 1::2] << 4)
    return np.ascontiguousarray(words), np.ascontiguousarray(byte.astype(np.uint8).reshape(k // 512, 16, n))


def unpack_weight(words, scales, fmt):
    g, p, n, _ = words.shape
    if fmt == "e4m3":
        vals = np.ascontiguousarray(words).view(ml_dtypes.float8_e4m3fn).astype(np.float64)
    else:
        nib = np.empty((g, p, n, 4), np.uint8)
        nib[..., 0::2] = words & 0xF
        nib[..., 1::2] = words >> 4
        vals = E2M1[nib]
    vals = vals * np.repeat(np.exp2(scales.astype(np.float64) - 127.0), 8, axis=1)[..., None]
    return vals.transpose(0, 1, 3, 2).reshape(g * 512, n)

def pack4(w):
    words, scales = pack_weight(w, "e2m1")
    return words.reshape(words.shape[0], 128, -1), scales


def unpack4(words, scales):
    return unpack_weight(words.reshape(words.shape[0], 128, -1, 2), scales, "e2m1")


def kspread(k):
    return np.exp2(np.repeat(np.random.randint(-6, 7, k // 32), 32).astype(np.float64))


B, I, H = 512, 2048, 1024
G = 2 * H
EPS = 1e-5


def ln(v):
    mu = v.mean(-1, keepdims=True)
    var = np.square(v - mu).mean(-1, keepdims=True)
    return (v - mu) / np.sqrt(var + EPS)


def sigmoid(v):
    return 1.0 / (1.0 + np.exp(-v))


def setup_inputs():
    s, t = kspread(I), kspread(H)
    x_words, x_scales = pack4((np.random.standard_normal((B, I)) * s).T)
    h_words, h_scales = pack4((np.random.standard_normal((B, H)) * t).T)
    irz_words, irz_scales = pack4((np.random.standard_normal((G, I)) / np.sqrt(I) / s).T)
    b_irz = bf(np.random.standard_normal(G) * 0.5)
    hrz_words, hrz_scales = pack4((np.random.standard_normal((G, H)) / np.sqrt(H) / t).T)
    b_hrz = bf(np.random.standard_normal(G) * 0.5)
    return {"x_words": x_words,
            "x_scales": x_scales,
            "h_words": h_words,
            "h_scales": h_scales,
            "W_irz_words": irz_words,
            "W_irz_scales": irz_scales,
            "b_irz": b_irz,
            "W_hrz_words": hrz_words,
            "W_hrz_scales": hrz_scales,
            "b_hrz": b_hrz}


def reference(x_words, x_scales, h_words, h_scales, W_irz_words, W_irz_scales, b_irz, W_hrz_words, W_hrz_scales, b_hrz):
    i_rz = ln((unpack4(x_words, x_scales).T @ unpack4(W_irz_words, W_irz_scales)) + f64(b_irz))
    h_rz = ln((unpack4(h_words, h_scales).T @ unpack4(W_hrz_words, W_hrz_scales)) + f64(b_hrz))
    return sigmoid(i_rz + h_rz)

@@ -1,0 +1,246 @@
+from contextlib import ExitStack
+
+import concourse.mybir as mybir
+
+F32 = mybir.dt.float32
+BF16 = mybir.dt.bfloat16
+I32 = mybir.dt.int32
+U8 = mybir.dt.uint8
+FP4X4 = mybir.dt.float4_e2m1fn_x4
+ALU = mybir.AluOpType
+ACT = mybir.ActivationFunctionType
+
+P = 128
+B, I, H = 512, 2048, 1024
+G = 2 * H
+EPS = 1e-5
+BANK = 512
+N_BANKS = G // BANK
+N_BLOCKS = B // P
+HALF = G // 2
+FLOPS = 2 * B * G * (I + H)
+
+
+def tile_layernormgrucell_pa_kernel(
+    tc, x_words, x_scales, h_words, h_scales, W_irz_words, W_irz_scales, b_irz,
+    W_hrz_words, W_hrz_scales, b_hrz, out,
+):
+    nc = tc.nc
+    with ExitStack() as ctx:
+        keep = ctx.enter_context(tc.tile_pool(name="keep", bufs=1))
+        junk_pool = ctx.enter_context(tc.tile_pool(name="junk", bufs=2))
+        psum = ctx.enter_context(tc.psum_pool(name="psum", bufs=8))
+        ctx.enter_context(tc.manual_schedule())
+
+        hw = keep.tile([P, 2, 2 * B], U8, name="hw", align_bytes=64)
+        xw = keep.tile([P, 4, 2 * B], U8, name="xw", align_bytes=64)
+        hp = keep.tile([P, 2, B], U8, name="hp", align_bytes=64)
+        xp = keep.tile([P, 4, B], U8, name="xp", align_bytes=64)
+        whw = [keep.tile([P, 2, 2 * HALF], U8, name=f"whw{c}", align_bytes=64) for c in range(2)]
+        wiw = [keep.tile([P, 4, 2 * HALF], U8, name=f"wiw{c}", align_bytes=64) for c in range(2)]
+        whp = keep.tile([P, 2, G], U8, name="whp", align_bytes=64)
+        wip = keep.tile([P, 4, G], U8, name="wip", align_bytes=64)
+
+        rows_h = keep.tile([P, BANK], BF16, name="rows_h", align_bytes=64)
+        rows_i = keep.tile([P, BANK], BF16, name="rows_i", align_bytes=64)
+        sel = keep.tile([P, N_BANKS], BF16, name="sel", align_bytes=64)
+        bias_h = keep.tile([P, G], BF16, name="bias_h", align_bytes=64)
+        bias_i = keep.tile([P, G], BF16, name="bias_i", align_bytes=64)
+        neg_half = keep.tile([P, N_BLOCKS], F32, name="neg_half", align_bytes=64)
+        neg_one = keep.tile([P, N_BLOCKS], F32, name="neg_one", align_bytes=64)
+        warm = keep.tile([P, 1], F32, name="warm", align_bytes=64)
+
+        def zero(engine, t):
+            flat = t[:].rearrange("p g n -> p (g n)") if len(t.shape) == 3 else t[:]
+            engine.memset(flat.bitcast(I32), 0)
+
+        zero(nc.vector, hp)
+        zero(nc.vector, whp)
+        zero(nc.gpsimd, rows_h)
+        nc.scalar.dma_start(out=rows_h[0:P:32, :], in_=b_hrz.rearrange("(c n) -> c n", c=N_BANKS))
+        zero(nc.gpsimd, rows_i)
+        nc.scalar.dma_start(out=rows_i[0:P:32, :], in_=b_irz.rearrange("(c n) -> c n", c=N_BANKS))
+        nc.gpsimd.memset(sel[:], 0.0)
+        for c in range(N_BANKS):
+            nc.gpsimd.memset(sel[32 * c : 32 * c + 1, c : c + 1], 1.0)
+        nc.gpsimd.memset(warm[:], 0.0)
+        nc.scalar.activation(out=warm[:], in_=warm[:], func=ACT.Sigmoid)
+        nc.gpsimd.memset(neg_half[:], -0.5)
+        nc.gpsimd.memset(neg_one[:], -1.0)
+        zero(nc.vector, xp)
+        zero(nc.vector, wip)
+
+        def load_words(t, src, g0, g1, c0, c1):
+            nc.sync.dma_start(out=t[:, g0:g1, :].bitcast(I32), in_=src[g0:g1, :, c0:c1].rearrange("g p c -> p g c").bitcast(I32))
+
+        def load_scales(t, src):
+            for q in range(4):
+                nc.sync.dma_start(
+                    out=t[32 * q : 32 * q + 4, :, :].bitcast(I32),
+                    in_=src[:, 4 * q : 4 * q + 4, :].rearrange("g r n -> r g n").bitcast(I32),
+                )
+
+        load_words(hw, h_words, 0, 2, 0, 2 * B)
+        load_words(whw[0], W_hrz_words, 0, 2, 0, 2 * HALF)
+        load_scales(hp, h_scales)
+        load_scales(whp, W_hrz_scales)
+        load_words(whw[1], W_hrz_words, 0, 2, 2 * HALF, 4 * HALF)
+        load_words(xw, x_words, 0, 4, 0, 2 * B)
+        load_scales(xp, x_scales)
+        load_scales(wip, W_irz_scales)
+        for c in range(2):
+            for g in (0, 2):
+                load_words(wiw[c], W_irz_words, g, g + 2, 2 * HALF * c, 2 * HALF * (c + 1))
+
+        def bias_bank(rows, dst, c, copy):
+            acc = psum.tile([P, 2 * BANK], BF16, name="acc")
+            for j in (0, 1):
+                nc.tensor.matmul(
+                    acc[:, BANK * j : BANK * (j + 1)], lhsT=sel[:, c + j : c + j + 1].to_broadcast([P, P]), rhs=rows[:], start=True, stop=True
+                )
+            copy(out=dst[:, BANK * c : BANK * (c + 2)], in_=acc[:])
+
+        def mm_bank(b, c0, w, aw, ap, ww, wp, passes):
+            acc = psum.tile([P, BANK], F32, name="acc")
+            lo = 2 * (c0 % HALF)
+            for g in range(passes):
+                nc.tensor.matmul_mx(
+                    out=acc[:, :w],
+                    lhsT=aw[:, g, 2 * P * b : 2 * P * (b + 1)].bitcast(FP4X4),
+                    lhsT_scale=ap[:, g, P * b : P * (b + 1)],
+                    rhs=ww[c0 // HALF][:, g, lo : lo + 2 * w].bitcast(FP4X4),
+                    rhs_scale=wp[:, g, c0 : c0 + w],
+                    start=(g == 0),
+                    stop=(g == passes - 1),
+                )
+            return acc
+
+        def col(t, j):
+            return t[:, j : j + 1]
+
+        gp = nc.gpsimd
+        h_ops = (hw, hp, whw, whp, 2)
+        i_ops = (xw, xp, wiw, wip, 4)
+        EPS_W = EPS * 128 * G * G
+        NB = N_BLOCKS
+
+        def f32(name, n):
+            return keep.tile([P, n], F32, name=name, align_bytes=64)
+
+        v_h = [f32(f"v_h{b}", G) for b in range(NB)]
+        v_i = [f32(f"v_i{b}", G) for b in range(NB)]
+        us = [f32(f"u{b}", G) for b in range(NB)]
+        s_h = f32("s_h", 4 * NB)
+        q_h = f32("q_h", 2 * NB)
+        t_h = f32("t_h", 12 * NB)
+        s_i = [f32(f"s_i{b}", 8) for b in range(NB)]
+        q_i = [f32(f"q_i{b}", 4) for b in range(NB)]
+        t_i = [f32(f"t_i{b}", 16) for b in range(NB)]
+
+        W4 = ((0, 512), (512, 1024), (1024, 1536), (1536, 2048))
+        W5 = ((0, 512), (512, 1024), (1024, 1536), (1536, 1792), (1792, 2048))
+        Q2 = ((0, 1024), (1024, 2048))
+
+        def bank(b, cols, v, s, bias, ops):
+            c0, c1 = cols
+            acc = mm_bank(b, c0, c1 - c0, *ops)
+            nc.vector.scalar_tensor_tensor(
+                out=v[:, c0:c1], in0=acc[:, : c1 - c0], scalar=1.0, in1=bias[:, c0:c1], op0=ALU.mult, op1=ALU.add, accum_out=s,
+            )
+
+        def squares(v, cols, s0, q):
+            c0, c1 = cols
+            junk = junk_pool.tile([P, HALF], BF16, name="junk")
+            nc.scalar.activation(out=junk[:, : c1 - c0], in_=v[:, c0:c1], func=ACT.Square, bias=s0, scale=-float(BANK), accum_out=q)
+
+        def add(out_, a, b2):
+            gp.tensor_tensor(out=out_, in0=a, in1=b2, op=ALU.add)
+
+        def fma(out_, a, m, c):
+            gp.tensor_scalar(out=out_, in0=a, scalar1=m, scalar2=c, op0=ALU.mult, op1=ALU.add)
+
+        def power(out_, a, e):
+            gp.tensor_tensor(out=out_, in0=a, in1=e, op=ALU.pow)
+
+        def th(j, b=None):
+            return t_h[:, NB * j : NB * (j + 1)] if b is None else col(t_h, NB * j + b)
+
+        def h_block(b):
+            for k in range(4):
+                bank(b, W4[k], v_h[b], col(s_h, NB * k + b), bias_h, h_ops)
+                if k % 2:
+                    squares(v_h[b], Q2[k // 2], col(s_h, b), col(q_h, NB * (k // 2) + b))
+
+        def h_stats():
+            add(t_h[:, 0 : 2 * NB], s_h[:, 0 : 2 * NB], s_h[:, 2 * NB : 4 * NB])
+            add(th(2), th(0), th(1))
+            fma(th(3), s_h[:, 0:NB], -4.0, 0.0)
+            add(th(3), th(3), th(2))
+            gp.tensor_tensor(out=th(4), in0=th(3), in1=th(3), op=ALU.mult)
+            fma(th(5), th(4), -128.0, EPS_W)
+            add(th(6), q_h[:, 0:NB], q_h[:, NB : 2 * NB])
+            add(th(7), th(6), th(5))
+            power(th(8), th(7), neg_one[:])
+            power(th(9), th(7), neg_half[:])
+            fma(th(10), th(9), G * 128**0.5, 0.0)
+            fma(th(11), th(9), -(128**0.5), 0.0)
+
+        def mix(b, c0, c1):
+            nc.vector.scalar_tensor_tensor(
+                out=us[b][:, c0:c1], in0=v_i[b][:, c0:c1], scalar=col(t_i[b], 6), in1=v_h[b][:, c0:c1], op0=ALU.mult, op1=ALU.add,
+            )
+
+        def sig(b, c0, c1):
+            nc.scalar.activation(out=us[b][:, c0:c1], in_=us[b][:, c0:c1], func=ACT.Sigmoid, bias=col(t_i[b], 8), scale=th(10, b))
+            nc.sync.dma_start(out=out[P * b : P * (b + 1), c0:c1], in_=us[b][:, c0:c1])
+
+        def i_block(b, mixes):
+            s, q, t = s_i[b], q_i[b], t_i[b]
+            last = b == NB - 1
+            banks = W5 if last else W4
+            pieces = Q2[:1] + banks[2:]
+            n = len(banks)
+            for k in range(n):
+                for a in mixes.get(k, ()):
+                    mix(*a)
+                bank(b, banks[k], v_i[b], col(s, k), bias_i, i_ops)
+                if k:
+                    squares(v_i[b], pieces[k - 1], col(s, 0), col(q, k - 1))
+                if k == 1:
+                    add(col(t, 0), col(s, 0), col(s, 1))
+                    fma(col(t, 1), col(s, 0), -4.0, col(t, 0))
+                elif k > 1:
+                    add(t[:, 0:2], t[:, 0:2], col(s, k).to_broadcast([P, 2]))
+            gp.tensor_tensor(out=col(t, 2), in0=col(t, 1), in1=col(t, 1), op=ALU.mult)
+            gp.tensor_scalar(out=col(t, 3), in0=col(q, 0), scalar1=EPS_W, scalar2=col(q, 1), op0=ALU.add, op1=ALU.add)
+            if last:
+                add(col(t, 3), col(t, 3), col(q, 2))
+            fma(col(t, 4), col(t, 2), -128.0, col(t, 3))
+            gp.tensor_scalar(out=col(t, 5), in0=col(q, n - 2), scalar1=col(t, 4), scalar2=th(8, b), op0=ALU.add, op1=ALU.mult)
+            power(col(t, 6), col(t, 5), neg_half[:, 0:1])
+            fma(col(t, 7), col(t, 0), col(t, 6), th(2, b))
+            gp.tensor_tensor(out=col(t, 8), in0=col(t, 7), in1=th(11, b), op=ALU.mult)
+            for a in mixes.get(n, ()):
+                mix(*a)
+
+        bias_bank(rows_h, bias_h, 0, nc.scalar.copy)
+        bias_bank(rows_h, bias_h, 2, nc.vector.tensor_copy)
+        bias_bank(rows_i, bias_i, 0, nc.scalar.copy)
+        bias_bank(rows_i, bias_i, 2, nc.scalar.copy)
+
+        for b in range(NB):
+            h_block(b)
+        h_stats()
+        i_block(0, {})
+        i_block(1, {4: ((0, 0, HALF), (0, HALF, G))})
+        sig(0, 0, HALF)
+        sig(0, HALF, G)
+        i_block(2, {3: ((1, 0, HALF),), 4: ((1, HALF, G),)})
+        sig(1, 0, HALF)
+        sig(1, HALF, G)
+        i_block(3, {5: ((2, 0, HALF), (2, HALF, G))})
+        sig(2, 0, HALF)
+        sig(2, HALF, G)
+        for c0, c1 in W5:
+            mix(3, c0, c1)
+            sig(3, c0, c1)

@@ -47,7 +47,6 @@ def tile_layernormgrucell_pa_kernel(
         bias_h = keep.tile([P, G], BF16, name="bias_h", align_bytes=64)
         bias_i = keep.tile([P, G], BF16, name="bias_i", align_bytes=64)
         neg_half = keep.tile([P, N_BLOCKS], F32, name="neg_half", align_bytes=64)
-        neg_one = keep.tile([P, N_BLOCKS], F32, name="neg_one", align_bytes=64)
         warm = keep.tile([P, 1], F32, name="warm", align_bytes=64)
 
         def zero(engine, t):
@@ -66,7 +65,6 @@ def tile_layernormgrucell_pa_kernel(
         nc.gpsimd.memset(warm[:], 0.0)
         nc.scalar.activation(out=warm[:], in_=warm[:], func=ACT.Sigmoid)
         nc.gpsimd.memset(neg_half[:], -0.5)
-        nc.gpsimd.memset(neg_one[:], -1.0)
         zero(nc.vector, xp)
         zero(nc.vector, wip)
 
@@ -119,10 +117,9 @@ def tile_layernormgrucell_pa_kernel(
             return t[:, j : j + 1]
 
         gp = nc.gpsimd
+        NB = N_BLOCKS
         h_ops = (hw, hp, whw, whp, 2)
         i_ops = (xw, xp, wiw, wip, 4)
-        EPS_W = EPS * 128 * G * G
-        NB = N_BLOCKS
 
         def f32(name, n):
             return keep.tile([P, n], F32, name=name, align_bytes=64)
@@ -130,117 +127,130 @@ def tile_layernormgrucell_pa_kernel(
         v_h = [f32(f"v_h{b}", G) for b in range(NB)]
         v_i = [f32(f"v_i{b}", G) for b in range(NB)]
         us = [f32(f"u{b}", G) for b in range(NB)]
-        s_h = f32("s_h", 4 * NB)
-        q_h = f32("q_h", 2 * NB)
-        t_h = f32("t_h", 12 * NB)
-        s_i = [f32(f"s_i{b}", 8) for b in range(NB)]
-        q_i = [f32(f"q_i{b}", 4) for b in range(NB)]
-        t_i = [f32(f"t_i{b}", 16) for b in range(NB)]
+        s_h = [f32(f"s_h{b}", N_BANKS) for b in range(NB)]
+        s_i = [f32(f"s_i{b}", N_BANKS) for b in range(NB)]
+        sum_h = f32("sum_h", NB)
+        dev_h = f32("dev_h", NB)
+        ve_h = f32("ve_h", NB)
+        r_h = f32("r_h", NB)
+        ir_h = f32("ir_h", NB)
+        rn_h = f32("rn_h", NB)
+        m_h = f32("m_h", NB)
+        nr_3 = f32("nr_3", 1)
+        sum_i = [f32(f"sum_i{b}", 1) for b in range(NB)]
+        dev_i = [f32(f"dev_i{b}", 1) for b in range(NB)]
+        t_i = [f32(f"t_i{b}", 3) for b in range(NB)]
+        a_i = [f32(f"a_i{b}", 1) for b in range(NB)]
+        c_i = [f32(f"c_i{b}", 1) for b in range(NB)]
+        bn = f32("bn", 6 * N_BANKS)
+        mv = f32("mv", 2)
 
-        W4 = ((0, 512), (512, 1024), (1024, 1536), (1536, 2048))
-        W5 = ((0, 512), (512, 1024), (1024, 1536), (1536, 1792), (1792, 2048))
-        Q2 = ((0, 1024), (1024, 2048))
+        def add_bias(b, k, v, bias, ops, s):
+            c0 = BANK * k
+            acc = mm_bank(b, c0, BANK, *ops)
+            if s is None:
+                nc.vector.tensor_tensor(out=v[:, c0 : c0 + BANK], in0=acc[:], in1=bias[:, c0 : c0 + BANK], op=ALU.add)
+            else:
+                nc.vector.scalar_tensor_tensor(
+                    out=v[:, c0 : c0 + BANK], in0=acc[:], scalar=1.0, in1=bias[:, c0 : c0 + BANK],
+                    op0=ALU.mult, op1=ALU.add, accum_out=col(s, k),
+                )
 
-        def bank(b, cols, v, s, bias, ops):
-            c0, c1 = cols
-            acc = mm_bank(b, c0, c1 - c0, *ops)
-            nc.vector.scalar_tensor_tensor(
-                out=v[:, c0:c1], in0=acc[:, : c1 - c0], scalar=1.0, in1=bias[:, c0:c1], op0=ALU.mult, op1=ALU.add, accum_out=s,
-            )
+        def a_h(b, k):
+            add_bias(b, k, v_h[b], bias_h, h_ops, s_h[b])
 
-        def squares(v, cols, s0, q):
-            c0, c1 = cols
-            junk = junk_pool.tile([P, HALF], BF16, name="junk")
-            nc.scalar.activation(out=junk[:, : c1 - c0], in_=v[:, c0:c1], func=ACT.Square, bias=s0, scale=-float(BANK), accum_out=q)
+        def a_i_(b, k):
+            add_bias(b, k, v_i[b], bias_i, i_ops, s_i[b] if b < NB - 1 else None)
 
-        def add(out_, a, b2):
-            gp.tensor_tensor(out=out_, in0=a, in1=b2, op=ALU.add)
+        def dev(v, s, total, q):
+            nc.vector.tensor_reduce(out=total, in_=s[:], axis=mybir.AxisListType.X, op=ALU.add)
+            junk = junk_pool.tile([P, G], BF16, name="junk")
+            nc.scalar.activation(out=junk[:], in_=v[:], func=ACT.Square, bias=total, scale=-float(G), accum_out=q)
 
-        def fma(out_, a, m, c):
+        def dev_hb(b):
+            dev(v_h[b], s_h[b], col(sum_h, b), col(dev_h, b))
+
+        def dev_ib(b):
+            dev(v_i[b], s_i[b], sum_i[b][:], dev_i[b][:])
+
+        def scale_add(out_, a, m, c):
             gp.tensor_scalar(out=out_, in0=a, scalar1=m, scalar2=c, op0=ALU.mult, op1=ALU.add)
 
-        def power(out_, a, e):
-            gp.tensor_tensor(out=out_, in0=a, in1=e, op=ALU.pow)
+        def mul(out_, a, b2):
+            gp.tensor_tensor(out=out_, in0=a, in1=b2, op=ALU.mult)
 
-        def th(j, b=None):
-            return t_h[:, NB * j : NB * (j + 1)] if b is None else col(t_h, NB * j + b)
+        def rsqrt(out_, a, n):
+            gp.tensor_tensor(out=out_, in0=a, in1=neg_half[:, :n], op=ALU.pow)
 
-        def h_block(b):
-            for k in range(4):
-                bank(b, W4[k], v_h[b], col(s_h, NB * k + b), bias_h, h_ops)
-                if k % 2:
-                    squares(v_h[b], Q2[k // 2], col(s_h, b), col(q_h, NB * (k // 2) + b))
+        def h_stats(b0, b1):
+            j = slice(b0, b1)
+            scale_add(ve_h[:, j], dev_h[:, j], 1.0 / G**3, EPS)
+            rsqrt(r_h[:, j], ve_h[:, j], b1 - b0)
+            mul(ir_h[:, j], r_h[:, j], r_h[:, j])
+            scale_add(rn_h[:, j], r_h[:, j], -1.0 / G, 0.0)
+            mul(m_h[:, j], sum_h[:, j], rn_h[:, j])
+            if b1 == NB:
+                scale_add(nr_3[:], col(r_h, NB - 1), -1.0, 0.0)
 
-        def h_stats():
-            add(t_h[:, 0 : 2 * NB], s_h[:, 0 : 2 * NB], s_h[:, 2 * NB : 4 * NB])
-            add(th(2), th(0), th(1))
-            fma(th(3), s_h[:, 0:NB], -4.0, 0.0)
-            add(th(3), th(3), th(2))
-            gp.tensor_tensor(out=th(4), in0=th(3), in1=th(3), op=ALU.mult)
-            fma(th(5), th(4), -128.0, EPS_W)
-            add(th(6), q_h[:, 0:NB], q_h[:, NB : 2 * NB])
-            add(th(7), th(6), th(5))
-            power(th(8), th(7), neg_one[:])
-            power(th(9), th(7), neg_half[:])
-            fma(th(10), th(9), G * 128**0.5, 0.0)
-            fma(th(11), th(9), -(128**0.5), 0.0)
+        def i_stats(b):
+            t = t_i[b]
+            if b < NB - 1:
+                scale_add(col(t, 0), dev_i[b][:], 1.0 / G**3, EPS)
+                mul(col(t, 1), col(t, 0), col(ir_h, b))
+            else:
+                gp.tensor_scalar(out=col(t, 1), in0=col(mv, 1), scalar1=EPS, scalar2=col(ir_h, b), op0=ALU.add, op1=ALU.mult)
+            rsqrt(col(t, 2), col(t, 1), 1)
+
+        def offset(b):
+            mean, r = (sum_i[b], col(rn_h, b)) if b < NB - 1 else (mv, nr_3[:])
+            nc.scalar.activation(out=a_i[b][:], in_=mean[:, 0:1], func=ACT.Identity, bias=0.0, scale=r)
+            nc.scalar.activation(out=c_i[b][:], in_=a_i[b][:], func=ACT.Identity, bias=col(m_h, b), scale=col(t_i[b], 2))
 
         def mix(b, c0, c1):
             nc.vector.scalar_tensor_tensor(
-                out=us[b][:, c0:c1], in0=v_i[b][:, c0:c1], scalar=col(t_i[b], 6), in1=v_h[b][:, c0:c1], op0=ALU.mult, op1=ALU.add,
+                out=us[b][:, c0:c1], in0=v_i[b][:, c0:c1], scalar=col(t_i[b], 2), in1=v_h[b][:, c0:c1], op0=ALU.mult, op1=ALU.add,
             )
 
         def sig(b, c0, c1):
-            nc.scalar.activation(out=us[b][:, c0:c1], in_=us[b][:, c0:c1], func=ACT.Sigmoid, bias=col(t_i[b], 8), scale=th(10, b))
+            nc.scalar.activation(out=us[b][:, c0:c1], in_=us[b][:, c0:c1], func=ACT.Sigmoid, bias=c_i[b][:], scale=col(r_h, b))
             nc.sync.dma_start(out=out[P * b : P * (b + 1), c0:c1], in_=us[b][:, c0:c1])
 
-        def i_block(b, mixes):
-            s, q, t = s_i[b], q_i[b], t_i[b]
-            last = b == NB - 1
-            banks = W5 if last else W4
-            pieces = Q2[:1] + banks[2:]
-            n = len(banks)
-            for k in range(n):
-                for a in mixes.get(k, ()):
-                    mix(*a)
-                bank(b, banks[k], v_i[b], col(s, k), bias_i, i_ops)
-                if k:
-                    squares(v_i[b], pieces[k - 1], col(s, 0), col(q, k - 1))
-                if k == 1:
-                    add(col(t, 0), col(s, 0), col(s, 1))
-                    fma(col(t, 1), col(s, 0), -4.0, col(t, 0))
-                elif k > 1:
-                    add(t[:, 0:2], t[:, 0:2], col(s, k).to_broadcast([P, 2]))
-            gp.tensor_tensor(out=col(t, 2), in0=col(t, 1), in1=col(t, 1), op=ALU.mult)
-            gp.tensor_scalar(out=col(t, 3), in0=col(q, 0), scalar1=EPS_W, scalar2=col(q, 1), op0=ALU.add, op1=ALU.add)
-            if last:
-                add(col(t, 3), col(t, 3), col(q, 2))
-            fma(col(t, 4), col(t, 2), -128.0, col(t, 3))
-            gp.tensor_scalar(out=col(t, 5), in0=col(q, n - 2), scalar1=col(t, 4), scalar2=th(8, b), op0=ALU.add, op1=ALU.mult)
-            power(col(t, 6), col(t, 5), neg_half[:, 0:1])
-            fma(col(t, 7), col(t, 0), col(t, 6), th(2, b))
-            gp.tensor_tensor(out=col(t, 8), in0=col(t, 7), in1=th(11, b), op=ALU.mult)
-            for a in mixes.get(n, ()):
-                mix(*a)
+        def bn_k(k):
+            nc.vector.bn_stats(out=bn[:, 6 * k : 6 * (k + 1)], in_=v_i[NB - 1][:, BANK * k : BANK * (k + 1)])
 
         bias_bank(rows_h, bias_h, 0, nc.scalar.copy)
         bias_bank(rows_h, bias_h, 2, nc.vector.tensor_copy)
         bias_bank(rows_i, bias_i, 0, nc.scalar.copy)
         bias_bank(rows_i, bias_i, 2, nc.scalar.copy)
 
-        for b in range(NB):
-            h_block(b)
-        h_stats()
-        i_block(0, {})
-        i_block(1, {4: ((0, 0, HALF), (0, HALF, G))})
-        sig(0, 0, HALF)
-        sig(0, HALF, G)
-        i_block(2, {3: ((1, 0, HALF),), 4: ((1, HALF, G),)})
-        sig(1, 0, HALF)
-        sig(1, HALF, G)
-        i_block(3, {5: ((2, 0, HALF), (2, HALF, G))})
-        sig(2, 0, HALF)
-        sig(2, HALF, G)
-        for c0, c1 in W5:
+        def four(f, b, after):
+            for k in range(N_BANKS):
+                f(b, k)
+                for g in after.get(k, ()):
+                    g()
+
+        def mixes(b):
+            for c0 in range(0, G, BANK):
+                mix(b, c0, c0 + BANK)
+
+        def sigs(b):
+            offset(b)
+            for c0 in (0, HALF):
+                sig(b, c0, c0 + HALF)
+
+        four(a_h, 0, {})
+        four(a_h, 1, {0: (lambda: dev_hb(0),)})
+        four(a_i_, 0, {0: (lambda: dev_hb(1), lambda: h_stats(0, 2))})
+        four(a_h, 2, {0: (lambda: dev_ib(0), lambda: i_stats(0))})
+        four(a_i_, 1, {0: (lambda: dev_hb(2), lambda: h_stats(2, 3)), 1: (lambda: mixes(0), lambda: sigs(0))})
+        four(a_h, 3, {0: (lambda: dev_ib(1), lambda: i_stats(1))})
+        four(a_i_, 2, {0: (lambda: dev_hb(3), lambda: h_stats(3, 4)), 2: (lambda: mixes(1), lambda: sigs(1))})
+        four(a_i_, 3, {0: (lambda: dev_ib(2), lambda: i_stats(2)), 1: (lambda: bn_k(0),), 2: (lambda: bn_k(1),), 3: (lambda: bn_k(2), lambda: bn_k(3))})
+        nc.vector.bn_aggr(out=mv[:], in_=bn[:])
+        i_stats(3)
+        mixes(2)
+        sigs(2)
+        offset(3)
+        for c0, c1 in ((0, 512), (512, 1024), (1024, 1536), (1536, 1792), (1792, 2048)):
             mix(3, c0, c1)
             sig(3, c0, c1)

@@ -53,12 +53,12 @@ def tile_layernormgrucell_pa_kernel(
             flat = t[:].rearrange("p g n -> p (g n)") if len(t.shape) == 3 else t[:]
             engine.memset(flat.bitcast(I32), 0)
 
-        zero(nc.vector, hp)
         zero(nc.vector, whp)
         zero(nc.gpsimd, rows_h)
         nc.scalar.dma_start(out=rows_h[0:P:32, :], in_=b_hrz.rearrange("(c n) -> c n", c=N_BANKS))
+        zero(nc.gpsimd, hp)
         zero(nc.gpsimd, rows_i)
-        nc.scalar.dma_start(out=rows_i[0:P:32, :], in_=b_irz.rearrange("(c n) -> c n", c=N_BANKS))
+        nc.gpsimd.dma_start(out=rows_i[0:P:32, :], in_=b_irz.rearrange("(c n) -> c n", c=N_BANKS))
         nc.gpsimd.memset(sel[:], 0.0)
         for c in range(N_BANKS):
             nc.gpsimd.memset(sel[32 * c : 32 * c + 1, c : c + 1], 1.0)
@@ -71,24 +71,24 @@ def tile_layernormgrucell_pa_kernel(
         def load_words(t, src, g0, g1, c0, c1):
             nc.sync.dma_start(out=t[:, g0:g1, :].bitcast(I32), in_=src[g0:g1, :, c0:c1].rearrange("g p c -> p g c").bitcast(I32))
 
-        def load_scales(t, src):
-            for q in range(4):
+        def load_scales(t, src, rows=(0, 1, 2, 3)):
+            for r in rows:
                 nc.sync.dma_start(
-                    out=t[32 * q : 32 * q + 4, :, :].bitcast(I32),
-                    in_=src[:, 4 * q : 4 * q + 4, :].rearrange("g r n -> r g n").bitcast(I32),
+                    out=t[r:P:32, :, :].bitcast(I32),
+                    in_=src[:, r:16:4, :].rearrange("g r n -> r g n").bitcast(I32),
                 )
 
+        load_scales(whp, W_hrz_scales, (0, 1))
         load_words(hw, h_words, 0, 2, 0, 2 * B)
         load_words(whw[0], W_hrz_words, 0, 2, 0, 2 * HALF)
+        load_scales(whp, W_hrz_scales, (2, 3))
         load_scales(hp, h_scales)
-        load_scales(whp, W_hrz_scales)
         load_words(whw[1], W_hrz_words, 0, 2, 2 * HALF, 4 * HALF)
-        load_words(xw, x_words, 0, 4, 0, 2 * B)
         load_scales(xp, x_scales)
+        load_words(xw, x_words, 0, 4, 0, 2 * B)
         load_scales(wip, W_irz_scales)
-        for c in range(2):
-            for g in (0, 2):
-                load_words(wiw[c], W_irz_words, g, g + 2, 2 * HALF * c, 2 * HALF * (c + 1))
+        load_words(wiw[0], W_irz_words, 0, 4, 0, 2 * HALF)
+        load_words(wiw[1], W_irz_words, 0, 4, 2 * HALF, 4 * HALF)
 
         def bias_bank(rows, dst, c, copy):
             acc = psum.tile([P, 2 * BANK], BF16, name="acc")
@@ -116,8 +116,8 @@ def tile_layernormgrucell_pa_kernel(
         def col(t, j):
             return t[:, j : j + 1]
 
-        gp = nc.gpsimd
         NB = N_BLOCKS
+        N3 = float(G) ** 3
         h_ops = (hw, hp, whw, whp, 2)
         i_ops = (xw, xp, wiw, wip, 4)
 
@@ -132,35 +132,31 @@ def tile_layernormgrucell_pa_kernel(
         sum_h = f32("sum_h", NB)
         dev_h = f32("dev_h", NB)
         ve_h = f32("ve_h", NB)
+        rs_h = f32("rs_h", NB)
+        iv_h = f32("iv_h", NB)
+        ie_h = f32("ie_h", NB)
         r_h = f32("r_h", NB)
-        ir_h = f32("ir_h", NB)
         rn_h = f32("rn_h", NB)
-        m_h = f32("m_h", NB)
-        nr_3 = f32("nr_3", 1)
         sum_i = [f32(f"sum_i{b}", 1) for b in range(NB)]
         dev_i = [f32(f"dev_i{b}", 1) for b in range(NB)]
-        t_i = [f32(f"t_i{b}", 3) for b in range(NB)]
-        a_i = [f32(f"a_i{b}", 1) for b in range(NB)]
+        w_i = [f32(f"w_i{b}", 1) for b in range(NB)]
+        rho = [f32(f"rho{b}", 1) for b in range(NB)]
+        y_i = [f32(f"y_i{b}", 1) for b in range(NB)]
         c_i = [f32(f"c_i{b}", 1) for b in range(NB)]
-        bn = f32("bn", 6 * N_BANKS)
-        mv = f32("mv", 2)
 
         def add_bias(b, k, v, bias, ops, s):
             c0 = BANK * k
             acc = mm_bank(b, c0, BANK, *ops)
-            if s is None:
-                nc.vector.tensor_tensor(out=v[:, c0 : c0 + BANK], in0=acc[:], in1=bias[:, c0 : c0 + BANK], op=ALU.add)
-            else:
-                nc.vector.scalar_tensor_tensor(
-                    out=v[:, c0 : c0 + BANK], in0=acc[:], scalar=1.0, in1=bias[:, c0 : c0 + BANK],
-                    op0=ALU.mult, op1=ALU.add, accum_out=col(s, k),
-                )
+            nc.vector.scalar_tensor_tensor(
+                out=v[:, c0 : c0 + BANK], in0=acc[:], scalar=1.0, in1=bias[:, c0 : c0 + BANK],
+                op0=ALU.mult, op1=ALU.add, accum_out=col(s, k),
+            )
 
         def a_h(b, k):
             add_bias(b, k, v_h[b], bias_h, h_ops, s_h[b])
 
-        def a_i_(b, k):
-            add_bias(b, k, v_i[b], bias_i, i_ops, s_i[b] if b < NB - 1 else None)
+        def a_i(b, k):
+            add_bias(b, k, v_i[b], bias_i, i_ops, s_i[b])
 
         def dev(v, s, total, q):
             nc.vector.tensor_reduce(out=total, in_=s[:], axis=mybir.AxisListType.X, op=ALU.add)
@@ -170,87 +166,108 @@ def tile_layernormgrucell_pa_kernel(
         def dev_hb(b):
             dev(v_h[b], s_h[b], col(sum_h, b), col(dev_h, b))
 
-        def dev_ib(b):
-            dev(v_i[b], s_i[b], sum_i[b][:], dev_i[b][:])
-
-        def scale_add(out_, a, m, c):
-            gp.tensor_scalar(out=out_, in0=a, scalar1=m, scalar2=c, op0=ALU.mult, op1=ALU.add)
-
-        def mul(out_, a, b2):
-            gp.tensor_tensor(out=out_, in0=a, in1=b2, op=ALU.mult)
-
-        def rsqrt(out_, a, n):
-            gp.tensor_tensor(out=out_, in0=a, in1=neg_half[:, :n], op=ALU.pow)
+        def affine(out_, a, scale, bias):
+            nc.scalar.activation(out=out_, in_=a, func=ACT.Identity, scale=scale, bias=bias)
 
         def h_stats(b0, b1):
             j = slice(b0, b1)
-            scale_add(ve_h[:, j], dev_h[:, j], 1.0 / G**3, EPS)
-            rsqrt(r_h[:, j], ve_h[:, j], b1 - b0)
-            mul(ir_h[:, j], r_h[:, j], r_h[:, j])
-            scale_add(rn_h[:, j], r_h[:, j], -1.0 / G, 0.0)
-            mul(m_h[:, j], sum_h[:, j], rn_h[:, j])
-            if b1 == NB:
-                scale_add(nr_3[:], col(r_h, NB - 1), -1.0, 0.0)
+            nc.gpsimd.tensor_scalar(out=ve_h[:, j], in0=dev_h[:, j], scalar1=1.0, scalar2=EPS * N3, op0=ALU.mult, op1=ALU.add)
+            nc.gpsimd.tensor_tensor(out=rs_h[:, j], in0=ve_h[:, j], in1=neg_half[:, j], op=ALU.pow)
+            nc.gpsimd.tensor_tensor(out=iv_h[:, j], in0=rs_h[:, j], in1=rs_h[:, j], op=ALU.mult)
+            nc.gpsimd.tensor_scalar(out=ie_h[:, j], in0=iv_h[:, j], scalar1=EPS * N3, scalar2=0.0, op0=ALU.mult, op1=ALU.add)
+
+        def h_factors(b0, b1):
+            j = slice(b0, b1)
+            affine(r_h[:, j], rs_h[:, j], N3**0.5, 0.0)
+            affine(rn_h[:, j], rs_h[:, j], -(G**0.5), 0.0)
 
         def i_stats(b):
-            t = t_i[b]
-            if b < NB - 1:
-                scale_add(col(t, 0), dev_i[b][:], 1.0 / G**3, EPS)
-                mul(col(t, 1), col(t, 0), col(ir_h, b))
-            else:
-                gp.tensor_scalar(out=col(t, 1), in0=col(mv, 1), scalar1=EPS, scalar2=col(ir_h, b), op0=ALU.add, op1=ALU.mult)
-            rsqrt(col(t, 2), col(t, 1), 1)
+            dev(v_i[b], s_i[b], sum_i[b][:], dev_i[b][:])
+            affine(w_i[b][:], dev_i[b][:], col(iv_h, b), col(ie_h, b))
+            nc.gpsimd.tensor_tensor(out=rho[b][:], in0=w_i[b][:], in1=neg_half[:, 0:1], op=ALU.pow)
 
         def offset(b):
-            mean, r = (sum_i[b], col(rn_h, b)) if b < NB - 1 else (mv, nr_3[:])
-            nc.scalar.activation(out=a_i[b][:], in_=mean[:, 0:1], func=ACT.Identity, bias=0.0, scale=r)
-            nc.scalar.activation(out=c_i[b][:], in_=a_i[b][:], func=ACT.Identity, bias=col(m_h, b), scale=col(t_i[b], 2))
+            affine(y_i[b][:], sum_i[b][:], rho[b][:], col(sum_h, b))
+            affine(c_i[b][:], y_i[b][:], col(rn_h, b), 0.0)
 
         def mix(b, c0, c1):
             nc.vector.scalar_tensor_tensor(
-                out=us[b][:, c0:c1], in0=v_i[b][:, c0:c1], scalar=col(t_i[b], 2), in1=v_h[b][:, c0:c1], op0=ALU.mult, op1=ALU.add,
+                out=us[b][:, c0:c1], in0=v_i[b][:, c0:c1], scalar=rho[b][:], in1=v_h[b][:, c0:c1], op0=ALU.mult, op1=ALU.add,
             )
 
         def sig(b, c0, c1):
             nc.scalar.activation(out=us[b][:, c0:c1], in_=us[b][:, c0:c1], func=ACT.Sigmoid, bias=c_i[b][:], scale=col(r_h, b))
             nc.sync.dma_start(out=out[P * b : P * (b + 1), c0:c1], in_=us[b][:, c0:c1])
 
-        def bn_k(k):
-            nc.vector.bn_stats(out=bn[:, 6 * k : 6 * (k + 1)], in_=v_i[NB - 1][:, BANK * k : BANK * (k + 1)])
-
         bias_bank(rows_h, bias_h, 0, nc.scalar.copy)
         bias_bank(rows_h, bias_h, 2, nc.vector.tensor_copy)
+        a_h(0, 0)
+        a_h(0, 1)
+        a_h(0, 2)
+        a_h(0, 3)
+        a_h(1, 0)
+        dev_hb(0)
+        a_h(1, 1)
+        a_h(1, 2)
+        a_h(1, 3)
         bias_bank(rows_i, bias_i, 0, nc.scalar.copy)
         bias_bank(rows_i, bias_i, 2, nc.scalar.copy)
-
-        def four(f, b, after):
-            for k in range(N_BANKS):
-                f(b, k)
-                for g in after.get(k, ()):
-                    g()
-
-        def mixes(b):
-            for c0 in range(0, G, BANK):
-                mix(b, c0, c0 + BANK)
-
-        def sigs(b):
-            offset(b)
-            for c0 in (0, HALF):
-                sig(b, c0, c0 + HALF)
-
-        four(a_h, 0, {})
-        four(a_h, 1, {0: (lambda: dev_hb(0),)})
-        four(a_i_, 0, {0: (lambda: dev_hb(1), lambda: h_stats(0, 2))})
-        four(a_h, 2, {0: (lambda: dev_ib(0), lambda: i_stats(0))})
-        four(a_i_, 1, {0: (lambda: dev_hb(2), lambda: h_stats(2, 3)), 1: (lambda: mixes(0), lambda: sigs(0))})
-        four(a_h, 3, {0: (lambda: dev_ib(1), lambda: i_stats(1))})
-        four(a_i_, 2, {0: (lambda: dev_hb(3), lambda: h_stats(3, 4)), 2: (lambda: mixes(1), lambda: sigs(1))})
-        four(a_i_, 3, {0: (lambda: dev_ib(2), lambda: i_stats(2)), 1: (lambda: bn_k(0),), 2: (lambda: bn_k(1),), 3: (lambda: bn_k(2), lambda: bn_k(3))})
-        nc.vector.bn_aggr(out=mv[:], in_=bn[:])
+        a_h(2, 0)
+        dev_hb(1)
+        a_h(2, 1)
+        a_h(2, 2)
+        a_h(2, 3)
+        a_h(3, 0)
+        dev_hb(2)
+        a_h(3, 1)
+        a_h(3, 2)
+        a_h(3, 3)
+        a_i(0, 0)
+        dev_hb(3)
+        h_stats(0, 4)
+        a_i(0, 1)
+        a_i(0, 2)
+        a_i(0, 3)
+        i_stats(0)
+        h_factors(0, 4)
+        offset(0)
+        a_i(1, 0)
+        a_i(1, 1)
+        a_i(1, 2)
+        a_i(1, 3)
+        i_stats(1)
+        mix(0, 0, 1024)
+        sig(0, 0, 1024)
+        mix(0, 1024, 2048)
+        sig(0, 1024, 2048)
+        offset(1)
+        a_i(2, 0)
+        a_i(2, 1)
+        a_i(2, 2)
+        a_i(2, 3)
+        i_stats(2)
+        mix(1, 0, 1024)
+        sig(1, 0, 1024)
+        mix(1, 1024, 2048)
+        sig(1, 1024, 2048)
+        offset(2)
+        a_i(3, 0)
+        a_i(3, 1)
+        a_i(3, 2)
+        a_i(3, 3)
         i_stats(3)
-        mixes(2)
-        sigs(2)
+        mix(2, 0, 1024)
+        sig(2, 0, 1024)
+        mix(2, 1024, 2048)
+        sig(2, 1024, 2048)
         offset(3)
-        for c0, c1 in ((0, 512), (512, 1024), (1024, 1536), (1536, 1792), (1792, 2048)):
-            mix(3, c0, c1)
-            sig(3, c0, c1)
+        mix(3, 0, 512)
+        sig(3, 0, 512)
+        mix(3, 512, 1024)
+        sig(3, 512, 1024)
+        mix(3, 1024, 1536)
+        sig(3, 1024, 1536)
+        mix(3, 1536, 1792)
+        sig(3, 1536, 1792)
+        mix(3, 1792, 2048)
+        sig(3, 1792, 2048)

from contextlib import ExitStack

import concourse.mybir as mybir

F32 = mybir.dt.float32
BF16 = mybir.dt.bfloat16
I32 = mybir.dt.int32
U8 = mybir.dt.uint8
FP4X4 = mybir.dt.float4_e2m1fn_x4
ALU = mybir.AluOpType
ACT = mybir.ActivationFunctionType

P = 128
B, I, H = 512, 2048, 1024
G = 2 * H
EPS = 1e-5
BANK = 512
N_BANKS = G // BANK
N_BLOCKS = B // P
HALF = G // 2
FLOPS = 2 * B * G * (I + H)


def tile_layernormgrucell_pa_kernel(
    tc, x_words, x_scales, h_words, h_scales, W_irz_words, W_irz_scales, b_irz,
    W_hrz_words, W_hrz_scales, b_hrz, out,
):
    nc = tc.nc
    with ExitStack() as ctx:
        keep = ctx.enter_context(tc.tile_pool(name="keep", bufs=1))
        junk_pool = ctx.enter_context(tc.tile_pool(name="junk", bufs=2))
        psum = ctx.enter_context(tc.psum_pool(name="psum", bufs=8))
        ctx.enter_context(tc.manual_schedule())

        hw = keep.tile([P, 2, 2 * B], U8, name="hw", align_bytes=64)
        xw = keep.tile([P, 4, 2 * B], U8, name="xw", align_bytes=64)
        hp = keep.tile([P, 2, B], U8, name="hp", align_bytes=64)
        xp = keep.tile([P, 4, B], U8, name="xp", align_bytes=64)
        whw = [keep.tile([P, 2, 2 * HALF], U8, name=f"whw{c}", align_bytes=64) for c in range(2)]
        wiw = [keep.tile([P, 4, 2 * HALF], U8, name=f"wiw{c}", align_bytes=64) for c in range(2)]
        whp = keep.tile([P, 2, G], U8, name="whp", align_bytes=64)
        wip = keep.tile([P, 4, G], U8, name="wip", align_bytes=64)

        rows_h = keep.tile([P, BANK], BF16, name="rows_h", align_bytes=64)
        rows_i = keep.tile([P, BANK], BF16, name="rows_i", align_bytes=64)
        sel = keep.tile([P, N_BANKS], BF16, name="sel", align_bytes=64)
        bias_h = keep.tile([P, G], BF16, name="bias_h", align_bytes=64)
        bias_i = keep.tile([P, G], BF16, name="bias_i", align_bytes=64)
        neg_half = keep.tile([P, N_BLOCKS], F32, name="neg_half", align_bytes=64)
        warm = keep.tile([P, 1], F32, name="warm", align_bytes=64)

        def zero(engine, t):
            flat = t[:].rearrange("p g n -> p (g n)") if len(t.shape) == 3 else t[:]
            engine.memset(flat.bitcast(I32), 0)

        zero(nc.vector, whp)
        zero(nc.gpsimd, rows_h)
        nc.scalar.dma_start(out=rows_h[0:P:32, :], in_=b_hrz.rearrange("(c n) -> c n", c=N_BANKS))
        zero(nc.gpsimd, hp)
        zero(nc.gpsimd, rows_i)
        nc.gpsimd.dma_start(out=rows_i[0:P:32, :], in_=b_irz.rearrange("(c n) -> c n", c=N_BANKS))
        nc.gpsimd.memset(sel[:], 0.0)
        for c in range(N_BANKS):
            nc.gpsimd.memset(sel[32 * c : 32 * c + 1, c : c + 1], 1.0)
        nc.gpsimd.memset(warm[:], 0.0)
        nc.scalar.activation(out=warm[:], in_=warm[:], func=ACT.Sigmoid)
        nc.gpsimd.memset(neg_half[:], -0.5)
        zero(nc.vector, xp)
        zero(nc.vector, wip)

        def load_words(t, src, g0, g1, c0, c1):
            nc.sync.dma_start(out=t[:, g0:g1, :].bitcast(I32), in_=src[g0:g1, :, c0:c1].rearrange("g p c -> p g c").bitcast(I32))

        def load_scales(t, src, rows=(0, 1, 2, 3)):
            for r in rows:
                nc.sync.dma_start(
                    out=t[r:P:32, :, :].bitcast(I32),
                    in_=src[:, r:16:4, :].rearrange("g r n -> r g n").bitcast(I32),
                )

        load_scales(whp, W_hrz_scales, (0, 1))
        load_words(hw, h_words, 0, 2, 0, 2 * B)
        load_words(whw[0], W_hrz_words, 0, 2, 0, 2 * HALF)
        load_scales(whp, W_hrz_scales, (2, 3))
        load_scales(hp, h_scales)
        load_words(whw[1], W_hrz_words, 0, 2, 2 * HALF, 4 * HALF)
        load_scales(xp, x_scales)
        load_words(xw, x_words, 0, 4, 0, 2 * B)
        load_scales(wip, W_irz_scales)
        load_words(wiw[0], W_irz_words, 0, 4, 0, 2 * HALF)
        load_words(wiw[1], W_irz_words, 0, 4, 2 * HALF, 4 * HALF)

        def bias_bank(rows, dst, c, copy):
            acc = psum.tile([P, 2 * BANK], BF16, name="acc")
            for j in (0, 1):
                nc.tensor.matmul(
                    acc[:, BANK * j : BANK * (j + 1)], lhsT=sel[:, c + j : c + j + 1].to_broadcast([P, P]), rhs=rows[:], start=True, stop=True
                )
            copy(out=dst[:, BANK * c : BANK * (c + 2)], in_=acc[:])

        def mm_bank(b, c0, w, aw, ap, ww, wp, passes):
            acc = psum.tile([P, BANK], F32, name="acc")
            lo = 2 * (c0 % HALF)
            for g in range(passes):
                nc.tensor.matmul_mx(
                    out=acc[:, :w],
                    lhsT=aw[:, g, 2 * P * b : 2 * P * (b + 1)].bitcast(FP4X4),
                    lhsT_scale=ap[:, g, P * b : P * (b + 1)],
                    rhs=ww[c0 // HALF][:, g, lo : lo + 2 * w].bitcast(FP4X4),
                    rhs_scale=wp[:, g, c0 : c0 + w],
                    start=(g == 0),
                    stop=(g == passes - 1),
                )
            return acc

        def col(t, j):
            return t[:, j : j + 1]

        NB = N_BLOCKS
        N3 = float(G) ** 3
        h_ops = (hw, hp, whw, whp, 2)
        i_ops = (xw, xp, wiw, wip, 4)

        def f32(name, n):
            return keep.tile([P, n], F32, name=name, align_bytes=64)

        v_h = [f32(f"v_h{b}", G) for b in range(NB)]
        v_i = [f32(f"v_i{b}", G) for b in range(NB)]
        us = [f32(f"u{b}", G) for b in range(NB)]
        s_h = [f32(f"s_h{b}", N_BANKS) for b in range(NB)]
        s_i = [f32(f"s_i{b}", N_BANKS) for b in range(NB)]
        sum_h = f32("sum_h", NB)
        dev_h = f32("dev_h", NB)
        ve_h = f32("ve_h", NB)
        rs_h = f32("rs_h", NB)
        iv_h = f32("iv_h", NB)
        ie_h = f32("ie_h", NB)
        r_h = f32("r_h", NB)
        rn_h = f32("rn_h", NB)
        sum_i = [f32(f"sum_i{b}", 1) for b in range(NB)]
        dev_i = [f32(f"dev_i{b}", 1) for b in range(NB)]
        w_i = [f32(f"w_i{b}", 1) for b in range(NB)]
        rho = [f32(f"rho{b}", 1) for b in range(NB)]
        y_i = [f32(f"y_i{b}", 1) for b in range(NB)]
        c_i = [f32(f"c_i{b}", 1) for b in range(NB)]

        def add_bias(b, k, v, bias, ops, s):
            c0 = BANK * k
            acc = mm_bank(b, c0, BANK, *ops)
            nc.vector.scalar_tensor_tensor(
                out=v[:, c0 : c0 + BANK], in0=acc[:], scalar=1.0, in1=bias[:, c0 : c0 + BANK],
                op0=ALU.mult, op1=ALU.add, accum_out=col(s, k),
            )

        def a_h(b, k):
            add_bias(b, k, v_h[b], bias_h, h_ops, s_h[b])

        def a_i(b, k):
            add_bias(b, k, v_i[b], bias_i, i_ops, s_i[b])

        def dev(v, s, total, q):
            nc.vector.tensor_reduce(out=total, in_=s[:], axis=mybir.AxisListType.X, op=ALU.add)
            junk = junk_pool.tile([P, G], BF16, name="junk")
            nc.scalar.activation(out=junk[:], in_=v[:], func=ACT.Square, bias=total, scale=-float(G), accum_out=q)

        def dev_hb(b):
            dev(v_h[b], s_h[b], col(sum_h, b), col(dev_h, b))

        def affine(out_, a, scale, bias):
            nc.scalar.activation(out=out_, in_=a, func=ACT.Identity, scale=scale, bias=bias)

        def h_stats(b0, b1):
            j = slice(b0, b1)
            nc.gpsimd.tensor_scalar(out=ve_h[:, j], in0=dev_h[:, j], scalar1=1.0, scalar2=EPS * N3, op0=ALU.mult, op1=ALU.add)
            nc.gpsimd.tensor_tensor(out=rs_h[:, j], in0=ve_h[:, j], in1=neg_half[:, j], op=ALU.pow)
            nc.gpsimd.tensor_tensor(out=iv_h[:, j], in0=rs_h[:, j], in1=rs_h[:, j], op=ALU.mult)
            nc.gpsimd.tensor_scalar(out=ie_h[:, j], in0=iv_h[:, j], scalar1=EPS * N3, scalar2=0.0, op0=ALU.mult, op1=ALU.add)

        def h_factors(b0, b1):
            j = slice(b0, b1)
            affine(r_h[:, j], rs_h[:, j], N3**0.5, 0.0)
            affine(rn_h[:, j], rs_h[:, j], -(G**0.5), 0.0)

        def i_stats(b):
            dev(v_i[b], s_i[b], sum_i[b][:], dev_i[b][:])
            affine(w_i[b][:], dev_i[b][:], col(iv_h, b), col(ie_h, b))
            nc.gpsimd.tensor_tensor(out=rho[b][:], in0=w_i[b][:], in1=neg_half[:, 0:1], op=ALU.pow)

        def offset(b):
            affine(y_i[b][:], sum_i[b][:], rho[b][:], col(sum_h, b))
            affine(c_i[b][:], y_i[b][:], col(rn_h, b), 0.0)

        def mix(b, c0, c1):
            nc.vector.scalar_tensor_tensor(
                out=us[b][:, c0:c1], in0=v_i[b][:, c0:c1], scalar=rho[b][:], in1=v_h[b][:, c0:c1], op0=ALU.mult, op1=ALU.add,
            )

        def sig(b, c0, c1):
            nc.scalar.activation(out=us[b][:, c0:c1], in_=us[b][:, c0:c1], func=ACT.Sigmoid, bias=c_i[b][:], scale=col(r_h, b))
            nc.sync.dma_start(out=out[P * b : P * (b + 1), c0:c1], in_=us[b][:, c0:c1])

        bias_bank(rows_h, bias_h, 0, nc.scalar.copy)
        bias_bank(rows_h, bias_h, 2, nc.vector.tensor_copy)
        a_h(0, 0)
        a_h(0, 1)
        a_h(0, 2)
        a_h(0, 3)
        a_h(1, 0)
        dev_hb(0)
        a_h(1, 1)
        a_h(1, 2)
        a_h(1, 3)
        bias_bank(rows_i, bias_i, 0, nc.scalar.copy)
        bias_bank(rows_i, bias_i, 2, nc.scalar.copy)
        a_h(2, 0)
        dev_hb(1)
        a_h(2, 1)
        a_h(2, 2)
        a_h(2, 3)
        a_h(3, 0)
        dev_hb(2)
        a_h(3, 1)
        a_h(3, 2)
        a_h(3, 3)
        a_i(0, 0)
        dev_hb(3)
        h_stats(0, 4)
        a_i(0, 1)
        a_i(0, 2)
        a_i(0, 3)
        i_stats(0)
        h_factors(0, 4)
        offset(0)
        a_i(1, 0)
        a_i(1, 1)
        a_i(1, 2)
        a_i(1, 3)
        i_stats(1)
        mix(0, 0, 1024)
        sig(0, 0, 1024)
        mix(0, 1024, 2048)
        sig(0, 1024, 2048)
        offset(1)
        a_i(2, 0)
        a_i(2, 1)
        a_i(2, 2)
        a_i(2, 3)
        i_stats(2)
        mix(1, 0, 1024)
        sig(1, 0, 1024)
        mix(1, 1024, 2048)
        sig(1, 1024, 2048)
        offset(2)
        a_i(3, 0)
        a_i(3, 1)
        a_i(3, 2)
        a_i(3, 3)
        i_stats(3)
        mix(2, 0, 1024)
        sig(2, 0, 1024)
        mix(2, 1024, 2048)
        sig(2, 1024, 2048)
        offset(3)
        mix(3, 0, 512)
        sig(3, 0, 512)
        mix(3, 512, 1024)
        sig(3, 512, 1024)
        mix(3, 1024, 1536)
        sig(3, 1024, 1536)
        mix(3, 1536, 1792)
        sig(3, 1536, 1792)
        mix(3, 1792, 2048)
        sig(3, 1792, 2048)
